import numpy as np
import ml_dtypes


def mxq(x, axis, fmt="e4m3"):
    dtype, down = {"e4m3": (ml_dtypes.float8_e4m3fn, 7), "e5m2": (ml_dtypes.float8_e5m2, 14)}[fmt]
    v = np.moveaxis(np.asarray(x, np.float32).astype(ml_dtypes.bfloat16).astype(np.float64), axis, -1)
    blocks = v.reshape(v.shape[:-1] + (-1, 32))
    amax = np.abs(blocks).max(-1, keepdims=True)
    byte = np.maximum(np.where(amax > 0, np.frexp(amax)[1] - 1 + 127, 0) - down, 1)
    scale = np.exp2(byte - 127.0)
    codes = (blocks / scale).astype(np.float32).astype(dtype).astype(np.float64)
    return np.moveaxis((codes * scale).reshape(v.shape), -1, axis)


WIDE = False


def mx_kscale(k):
    if not WIDE:
        return np.ones(k)
    levels = np.array([30, -30])
    if k % 512:
        return np.exp2(np.random.permutation(np.resize(levels, k // 32))).repeat(32)
    a = np.empty((k // 512, 16))
    for p in range(k // 512):
        a[p, :8] = np.random.permutation(np.resize(levels, 8))
        for g in range(8):
            far = levels[np.abs(levels - a[p, g]) >= 10]
            a[p, g + 8] = far[np.random.randint(len(far))]
    return np.exp2(a.ravel()).repeat(32)


BF16 = ml_dtypes.bfloat16


def bf(x):
    return np.asarray(x, np.float32).astype(BF16)


def f64(x):
    return np.asarray(x).astype(np.float64)


B, T, C, NH, NKV, HD, P = 1, 512, 2048, 16, 4, 128, 512


def rope(u, angles):
    up = u.reshape(u.shape[:-1] + (HD // 2, 2))
    cos = np.cos(angles)[None, :, None, :]
    sin = np.sin(angles)[None, :, None, :]
    u0, u1 = up[..., 0], up[..., 1]
    return np.stack([cos * u0 - sin * u1, sin * u0 + cos * u1], axis=-1).reshape(u.shape)


def setup_inputs():
    s = mx_kscale(C)
    return {"x": bf(np.random.standard_normal((B, T, C)) * s),
            "angles": bf(np.random.uniform(-np.pi, np.pi, (T, HD // 2))),
            "wq": bf(np.random.standard_normal((C, NH * HD)) * 0.5 / np.sqrt(C) / s[:, None]),
            "wk": bf(np.random.standard_normal((C, NKV * HD)) * 0.5 / np.sqrt(C) / s[:, None]),
            "wv": bf(np.random.standard_normal((C, NKV * HD)) / np.sqrt(C) / s[:, None])}


def reference(x, angles, wq, wk, wv):
    xq = mxq(f64(x), 2, "e5m2")
    a = f64(angles)
    q = (xq @ mxq(f64(wq), 0, "e4m3")).reshape(B, T, NH, HD)
    k = (xq @ mxq(f64(wk), 0, "e4m3")).reshape(B, T, NKV, HD)
    v = (xq @ mxq(f64(wv), 0, "e4m3")).reshape(B, T, NKV, HD)
    q = rope(q, a)
    k = rope(k, a)
    return q.transpose(0, 2, 1, 3), k.transpose(0, 2, 1, 3), v.transpose(0, 2, 1, 3)

@@ -1,0 +1,283 @@
+import math
+from contextlib import ExitStack
+
+import concourse.mybir as mybir
+from concourse.masks import make_identity
+
+F32 = mybir.dt.float32
+BF16 = mybir.dt.bfloat16
+U32 = mybir.dt.uint32
+U8 = mybir.dt.uint8
+E4M3X4 = mybir.dt.float8_e4m3fn_x4
+E5M2X4 = mybir.dt.float8_e5m2_x4
+ALU = mybir.AluOpType
+ACT = mybir.ActivationFunctionType
+
+T, C, HD = 512, 2048, 128
+FLOPS = 2 * T * C * 3072
+
+P = 128
+PACK = 4
+K_PASS = P * PACK
+PASSES = C // K_PASS
+TILES = T // P
+CHUNK = 512
+HEADS = CHUNK // HD
+CHUNKS = 6
+RUN = 4
+
+HEAD_SHARE = 320
+BRIDGE_SHARE = 256
+STEADY_SHARE = 192
+POOL_HEADS = 3
+
+
+def tile_groupqueryatention_pa_kernel(tc, x, angles, wq, wk, wv, out_0, out_1, out_2):
+    nc = tc.nc
+    x_rows = x[0].rearrange("(p j) k -> j p k", j=TILES)
+    dests = [out_1[0]] + [out_0[0, HEADS * i : HEADS * (i + 1)] for i in range(4)] + [out_2[0]]
+
+    with ExitStack() as ctx:
+        keep = ctx.enter_context(tc.tile_pool(name="keep", bufs=1))
+        grouped_pool = ctx.enter_context(tc.tile_pool(name="grouped", bufs=5))
+        codes_pool = ctx.enter_context(tc.tile_pool(name="codes", bufs=6))
+        psum = ctx.enter_context(tc.psum_pool(name="psum", bufs=1))
+        ctx.enter_context(tc.manual_schedule())
+
+        raw_w = {}
+        raw_x = {}
+
+        def load_w(w, g, col0, chunks):
+            width = CHUNK * len(chunks)
+            raw = keep.tile([P, PACK, width], BF16, name="raw_w_%d_%d" % (chunks[0], g))
+            rows = w[g * K_PASS : (g + 1) * K_PASS, col0 : col0 + width]
+            nc.sync.dma_start(out=raw[:], in_=rows.rearrange("(p t) n -> p t n", t=PACK))
+            for i, c in enumerate(chunks):
+                raw_w[c, g] = raw[:, :, i * CHUNK : (i + 1) * CHUNK]
+
+        def load_x(j):
+            raw = keep.tile([P, C], BF16, name="raw_x_%d" % j)
+            nc.sync.dma_start(out=raw[:], in_=x_rows[j])
+            raw_x[j] = raw
+
+        ang = keep.tile([P, TILES * HD // 2], BF16)
+        nc.sync.dma_start(out=ang[:], in_=angles.rearrange("(p j) i -> p (j i)", j=TILES))
+        load_w(wk, 0, 0, [0])
+        load_x(0)
+        for s in range(1, PASSES):
+            load_x(s)
+            load_w(wk, s, 0, [0])
+        load_w(wq, 0, 0, [1])
+        for g in range(1, PASSES):
+            load_w(wq, g, 0, [1, 2])
+        load_w(wq, 0, CHUNK, [2])
+        for g in range(PASSES):
+            load_w(wq, g, 2 * CHUNK, [3, 4])
+        for g in range(PASSES):
+            load_w(wv, g, 0, [5])
+
+        ident = keep.tile([P, P], F32)
+        make_identity(nc, ident[:])
+
+        pairs = TILES * HD // 2
+        signs = keep.tile([P, 2], F32)
+        nc.vector.memset(signs[:, 0:1], -1.0)
+        nc.vector.memset(signs[:, 1:2], 1.0)
+        magnitude = keep.tile([P, pairs], F32)
+        phases = keep.tile([P, 2, pairs, 2], F32)
+        nc.vector.scalar_tensor_tensor(
+            out=magnitude[:], in0=ang[:], scalar=-1.0, in1=ang[:], op0=ALU.mult, op1=ALU.max
+        )
+        nc.vector.tensor_tensor(
+            out=phases[:, 1],
+            in0=ang[:].unsqueeze(2).to_broadcast([P, pairs, 2]),
+            in1=signs[:].unsqueeze(1).to_broadcast([P, pairs, 2]),
+            op=ALU.mult,
+        )
+        nc.vector.tensor_scalar(
+            out=phases[:, 0],
+            in0=magnitude[:].unsqueeze(2).to_broadcast([P, pairs, 2]),
+            scalar1=-1.0,
+            scalar2=math.pi / 2,
+            op0=ALU.mult,
+            op1=ALU.add,
+        )
+        trig = keep.tile([P, 2, TILES, HD], F32)
+        nc.scalar.activation(
+            out=trig[:].rearrange("p a j d -> p (a j d)"),
+            in_=phases[:].rearrange("p a i e -> p (a i e)"),
+            func=ACT.Sin,
+        )
+
+        grouped_w = {}
+        codes_w = {}
+        grouped_x = {}
+        codes_x = {}
+        acc = {}
+        stage = {}
+        swapped = keep.tile([P, HEADS, TILES, HD], F32)
+
+        def share(c, g):
+            if c == 0:
+                return HEAD_SHARE
+            if (c, g) == (1, 0):
+                return BRIDGE_SHARE
+            return STEADY_SHARE if g == PASSES - 1 else 0
+
+        def grouped_tile(c, g):
+            if (c, g) not in grouped_w:
+                grouped_w[c, g] = grouped_pool.tile(
+                    [P, CHUNK, PACK], BF16, name="grouped", tag="grouped", align_bytes=64
+                )
+            return grouped_w[c, g]
+
+        def interleave_views(c, g, lo, hi):
+            dst = grouped_tile(c, g)[:, lo:hi, :].rearrange("p (n i) t -> p n t i", i=RUN)
+            src = raw_w[c, g][:, :, lo:hi].rearrange("p t (n i) -> p n t i", i=RUN)
+            return dst, src
+
+        def interleave_vector(c, g):
+            dst, src = interleave_views(c, g, 0, share(c, g))
+            nc.vector.tensor_copy(out=dst, in_=src)
+
+        def interleave_scalar(c, g):
+            dst, src = interleave_views(c, g, share(c, g), CHUNK)
+            nc.scalar.copy(out=dst, in_=src)
+
+        def quantize_w(c, g):
+            codes = codes_pool.tile([P, CHUNK], U32, name="w_codes", tag="w_codes", align_bytes=64)
+            scales = codes_pool.tile([P, CHUNK], U8, name="w_scales", tag="w_scales", align_bytes=64)
+            nc.vector.quantize_mx(
+                out=codes[:].bitcast(E4M3X4),
+                scales=scales[:],
+                in_=grouped_w[c, g][:].rearrange("p n t -> p (n t)"),
+            )
+            codes_w[c, g] = (codes, scales)
+
+        def transpose_x(j):
+            words = raw_x[j][:].bitcast(F32)
+            grouped = grouped_pool.tile([P, C], BF16, name="grouped", tag="grouped", align_bytes=64)
+            grouped_x[j] = grouped
+            for b in range(2):
+                xt = psum.tile([P, 2, 2, P], F32, name="xt", tag="bank%d" % (TILES + 2 * (j % 2) + b))
+                for h in range(2):
+                    g = 2 * b + h
+                    for u in range(2):
+                        nc.tensor.transpose(
+                            xt[:, h, u, :], words[:, 256 * g + u : 256 * (g + 1) : 2], ident[:]
+                        )
+                dst = grouped[:].bitcast(F32)[:, 512 * b : 512 * (b + 1)]
+                nc.scalar.copy(
+                    out=dst.rearrange("p (h r u) -> p h r u", h=2, u=2),
+                    in_=xt[:].rearrange("p h u r -> p h r u"),
+                )
+
+        def quantize_x(j):
+            codes = keep.tile([P, PASSES * P], U32, name="x_codes_%d" % j, align_bytes=64)
+            scales = keep.tile([P, PASSES * P], U8, name="x_scales_%d" % j, align_bytes=64)
+            nc.vector.quantize_mx(out=codes[:].bitcast(E5M2X4), scales=scales[:], in_=grouped_x[j][:])
+            codes_x[j] = (codes, scales)
+
+        def multiply(c, g, j):
+            if g == 0:
+                acc[c, j] = psum.tile([P, CHUNK], F32, name="acc", tag="bank%d" % (TILES * (c % 2) + j))
+            x_codes, x_scales = codes_x[j]
+            w_codes, w_scales = codes_w[c, g]
+            cols = slice(g * P, (g + 1) * P)
+            nc.tensor.matmul_mx(
+                out=acc[c, j][:],
+                lhsT=x_codes[:, cols].bitcast(E5M2X4),
+                lhsT_scale=x_scales[:, cols],
+                rhs=w_codes[:].bitcast(E4M3X4),
+                rhs_scale=w_scales[:],
+                start=(g == 0),
+                stop=(g == PASSES - 1),
+            )
+
+        def quantize_and_multiply(c, g):
+            quantize_w(c, g)
+            for j in range(TILES):
+                multiply(c, g, j)
+
+        def stage_tile(c):
+            stage[c] = keep.tile([P, HEADS, TILES, HD], F32, name="stage_%d" % c)
+
+        def rope_products(c, j):
+            shape = [P, HEADS, HD // 2, 2]
+            sums = acc[c, j][:].rearrange("p (h i e) -> p h i e", h=HEADS, e=2)
+            cos = trig[:, 0, j, :].rearrange("p (i e) -> p i e", e=2).unsqueeze(1).to_broadcast(shape)
+            sin = trig[:, 1, j, :].rearrange("p (i e) -> p i e", e=2).unsqueeze(1).to_broadcast(shape)
+            nc.vector.tensor_tensor(
+                out=stage[c][:, :, j, :].rearrange("p h (i e) -> p h i e", e=2),
+                in0=sums,
+                in1=cos,
+                op=ALU.mult,
+            )
+            nc.vector.tensor_tensor(
+                out=swapped[:, :, j, :].rearrange("p h (i e) -> p h i e", e=2),
+                in0=sums[:, :, :, ::-1],
+                in1=sin,
+                op=ALU.mult,
+            )
+
+        def rope_add(engine, c, heads, tiles):
+            part = stage[c][:, heads, tiles, :]
+            engine.tensor_tensor(out=part, in0=part, in1=swapped[:, heads, tiles, :], op=ALU.add)
+
+        def store(c, tiles):
+            dst = dests[c].rearrange("h (p j) d -> p h j d", j=TILES)[:, :, tiles, :]
+            nc.sync.dma_start(
+                out=dst.rearrange("p h j d -> p h (j d)"),
+                in_=stage[c][:, :, tiles, :].rearrange("p h j d -> p h (j d)"),
+            )
+
+        interleave_vector(0, 0)
+        interleave_scalar(0, 0)
+        quantize_w(0, 0)
+        transpose_x(0)
+        for s in range(1, PASSES):
+            transpose_x(s)
+            interleave_vector(0, s)
+            interleave_scalar(0, s)
+            quantize_x(s - 1)
+            quantize_w(0, s)
+        interleave_vector(1, 0)
+        interleave_scalar(1, 0)
+        quantize_x(TILES - 1)
+        for j in range(TILES):
+            for g in range(PASSES):
+                multiply(0, g, j)
+        quantize_and_multiply(1, 0)
+
+        last = TILES - 1
+        for c in range(1, CHUNKS):
+            done = c - 1
+            interleave_scalar(c, 1)
+            interleave_scalar(c, 2)
+            stage_tile(done)
+            for j in range(TILES):
+                rope_products(done, j)
+                if j < last:
+                    rope_add(nc.gpsimd, done, slice(0, POOL_HEADS), slice(j, j + 1))
+            quantize_and_multiply(c, 1)
+            interleave_vector(c, 3)
+            interleave_scalar(c, 3)
+            quantize_and_multiply(c, 2)
+            quantize_and_multiply(c, 3)
+            rope_add(nc.vector, done, slice(POOL_HEADS, HEADS), slice(0, last))
+            rope_add(nc.vector, done, slice(0, HEADS), slice(last, TILES))
+            store(done, slice(0, TILES))
+            if c + 1 < CHUNKS:
+                interleave_scalar(c + 1, 0)
+                quantize_and_multiply(c + 1, 0)
+
+        c = CHUNKS - 1
+        stage_tile(c)
+        for j in range(TILES):
+            sums = acc[c, j][:].rearrange("p (h d) -> p h d", h=HEADS)
+            if j < 2:
+                nc.scalar.copy(out=stage[c][:, :, j, :], in_=sums)
+            else:
+                nc.vector.tensor_copy(out=stage[c][:, :, j, :], in_=sums)
+            if j % 2 == 1:
+                store(c, slice(j - 1, j + 1))

@@ -29,7 +29,7 @@ RUN = 4
 HEAD_SHARE = 320
 BRIDGE_SHARE = 256
 STEADY_SHARE = 192
-POOL_HEADS = 3
+POOL_TILES = 2
 
 
 def tile_groupqueryatention_pa_kernel(tc, x, angles, wq, wk, wv, out_0, out_1, out_2):
@@ -67,10 +67,9 @@ def tile_groupqueryatention_pa_kernel(tc, x, angles, wq, wk, wv, out_0, out_1, o
         for s in range(1, PASSES):
             load_x(s)
             load_w(wk, s, 0, [0])
-        load_w(wq, 0, 0, [1])
-        for g in range(1, PASSES):
-            load_w(wq, g, 0, [1, 2])
-        load_w(wq, 0, CHUNK, [2])
+        for c in (1, 2):
+            for g in range(PASSES):
+                load_w(wq, g, (c - 1) * CHUNK, [c])
         for g in range(PASSES):
             load_w(wq, g, 2 * CHUNK, [3, 4])
         for g in range(PASSES):
@@ -220,9 +219,9 @@ def tile_groupqueryatention_pa_kernel(tc, x, angles, wq, wk, wv, out_0, out_1, o
                 op=ALU.mult,
             )
 
-        def rope_add(engine, c, heads, tiles):
-            part = stage[c][:, heads, tiles, :]
-            engine.tensor_tensor(out=part, in0=part, in1=swapped[:, heads, tiles, :], op=ALU.add)
+        def rope_add(engine, c, tiles):
+            part = stage[c][:, :, tiles, :]
+            engine.tensor_tensor(out=part, in0=part, in1=swapped[:, :, tiles, :], op=ALU.add)
 
         def store(c, tiles):
             dst = dests[c].rearrange("h (p j) d -> p h j d", j=TILES)[:, :, tiles, :]
@@ -241,43 +240,60 @@ def tile_groupqueryatention_pa_kernel(tc, x, angles, wq, wk, wv, out_0, out_1, o
             interleave_scalar(0, s)
             quantize_x(s - 1)
             quantize_w(0, s)
+        quantize_x(TILES - 1)
         interleave_vector(1, 0)
         interleave_scalar(1, 0)
-        quantize_x(TILES - 1)
-        for j in range(TILES):
+        for j in range(2):
+            for g in range(PASSES - 1):
+                multiply(0, g, j)
+        for j in range(2):
+            multiply(0, PASSES - 1, j)
+        for j in range(2, TILES):
             for g in range(PASSES):
                 multiply(0, g, j)
         quantize_and_multiply(1, 0)
 
-        last = TILES - 1
-        for c in range(1, CHUNKS):
-            done = c - 1
-            interleave_scalar(c, 1)
-            interleave_scalar(c, 2)
-            stage_tile(done)
+        def rope_run(c):
+            interleave_scalar(c + 1, 1)
+            interleave_scalar(c + 1, 2)
+            stage_tile(c)
             for j in range(TILES):
-                rope_products(done, j)
-                if j < last:
-                    rope_add(nc.gpsimd, done, slice(0, POOL_HEADS), slice(j, j + 1))
+                rope_products(c, j)
+                if j < POOL_TILES:
+                    rope_add(nc.gpsimd, c, slice(j, j + 1))
+
+        for c in range(1, CHUNKS - 1):
+            done = c - 1
+            rope_run(done)
             quantize_and_multiply(c, 1)
             interleave_vector(c, 3)
             interleave_scalar(c, 3)
-            quantize_and_multiply(c, 2)
-            quantize_and_multiply(c, 3)
-            rope_add(nc.vector, done, slice(POOL_HEADS, HEADS), slice(0, last))
-            rope_add(nc.vector, done, slice(0, HEADS), slice(last, TILES))
+            quantize_w(c, 2)
+            quantize_w(c, 3)
+            for j in range(TILES):
+                multiply(c, 2, j)
+                multiply(c, 3, j)
+            rope_add(nc.vector, done, slice(POOL_TILES, TILES))
             store(done, slice(0, TILES))
-            if c + 1 < CHUNKS:
-                interleave_scalar(c + 1, 0)
-                quantize_and_multiply(c + 1, 0)
+            interleave_scalar(c + 1, 0)
+            quantize_and_multiply(c + 1, 0)
 
         c = CHUNKS - 1
+        done = c - 1
+        rope_run(done)
+        store(done, slice(0, POOL_TILES))
+        quantize_and_multiply(c, 1)
+        rope_add(nc.vector, done, slice(POOL_TILES, TILES))
+        store(done, slice(POOL_TILES, TILES))
+        interleave_vector(c, 3)
+        interleave_scalar(c, 3)
+        quantize_and_multiply(c, 2)
+        quantize_and_multiply(c, 3)
         stage_tile(c)
         for j in range(TILES):
             sums = acc[c, j][:].rearrange("p (h d) -> p h d", h=HEADS)
-            if j < 2:
+            if j % 2 == 0:
                 nc.scalar.copy(out=stage[c][:, :, j, :], in_=sums)
             else:
                 nc.vector.tensor_copy(out=stage[c][:, :, j, :], in_=sums)
-            if j % 2 == 1:
                 store(c, slice(j - 1, j + 1))

@@ -27,7 +27,13 @@ CHUNKS = 6
 RUN = 4
 
 HEAD_SHARE = 320
-BRIDGE_SHARE = 256
+BRIDGE_SHARE = 384
+HEAD_LAST_SHARE = 384
+TAIL_SHARE = 128
+GB = 6
+ADDAT = 2
+EVAT = 3
+EARLY = 3
 STEADY_SHARE = 192
 POOL_TILES = 2
 
@@ -35,11 +41,14 @@ POOL_TILES = 2
 def tile_groupqueryatention_pa_kernel(tc, x, angles, wq, wk, wv, out_0, out_1, out_2):
     nc = tc.nc
     x_rows = x[0].rearrange("(p j) k -> j p k", j=TILES)
-    dests = [out_1[0]] + [out_0[0, HEADS * i : HEADS * (i + 1)] for i in range(4)] + [out_2[0]]
+    dests = [out_1[0]] + [out_0[0, HEADS * i : HEADS * (i + 1)] for i in range(4)]
+    dests += [out_2[0, 0:2], out_2[0, 2:4]]
+    bank_set = [0, 1, 0, 1, 0, 0, 1]
+    widths = [CHUNK] * 5 + [CHUNK // 2] * 2
 
     with ExitStack() as ctx:
         keep = ctx.enter_context(tc.tile_pool(name="keep", bufs=1))
-        grouped_pool = ctx.enter_context(tc.tile_pool(name="grouped", bufs=5))
+        grouped_pool = ctx.enter_context(tc.tile_pool(name="grouped", bufs=GB))
         codes_pool = ctx.enter_context(tc.tile_pool(name="codes", bufs=6))
         psum = ctx.enter_context(tc.psum_pool(name="psum", bufs=1))
         ctx.enter_context(tc.manual_schedule())
@@ -48,12 +57,12 @@ def tile_groupqueryatention_pa_kernel(tc, x, angles, wq, wk, wv, out_0, out_1, o
         raw_x = {}
 
         def load_w(w, g, col0, chunks):
-            width = CHUNK * len(chunks)
+            width = sum(widths[c] for c in chunks)
             raw = keep.tile([P, PACK, width], BF16, name="raw_w_%d_%d" % (chunks[0], g))
             rows = w[g * K_PASS : (g + 1) * K_PASS, col0 : col0 + width]
             nc.sync.dma_start(out=raw[:], in_=rows.rearrange("(p t) n -> p t n", t=PACK))
             for i, c in enumerate(chunks):
-                raw_w[c, g] = raw[:, :, i * CHUNK : (i + 1) * CHUNK]
+                raw_w[c, g] = raw[:, :, i * widths[c] : (i + 1) * widths[c]]
 
         def load_x(j):
             raw = keep.tile([P, C], BF16, name="raw_x_%d" % j)
@@ -62,9 +71,7 @@ def tile_groupqueryatention_pa_kernel(tc, x, angles, wq, wk, wv, out_0, out_1, o
 
         ang = keep.tile([P, TILES * HD // 2], BF16)
         nc.sync.dma_start(out=ang[:], in_=angles.rearrange("(p j) i -> p (j i)", j=TILES))
-        load_w(wk, 0, 0, [0])
-        load_x(0)
-        for s in range(1, PASSES):
+        for s in range(PASSES):
             load_x(s)
             load_w(wk, s, 0, [0])
         for c in (1, 2):
@@ -73,7 +80,7 @@ def tile_groupqueryatention_pa_kernel(tc, x, angles, wq, wk, wv, out_0, out_1, o
         for g in range(PASSES):
             load_w(wq, g, 2 * CHUNK, [3, 4])
         for g in range(PASSES):
-            load_w(wv, g, 0, [5])
+            load_w(wv, g, 0, [5, 6])
 
         ident = keep.tile([P, P], F32)
         make_identity(nc, ident[:])
@@ -82,30 +89,33 @@ def tile_groupqueryatention_pa_kernel(tc, x, angles, wq, wk, wv, out_0, out_1, o
         signs = keep.tile([P, 2], F32)
         nc.vector.memset(signs[:, 0:1], -1.0)
         nc.vector.memset(signs[:, 1:2], 1.0)
+        sine = keep.tile([P, pairs], F32)
+        nc.scalar.activation(out=sine[:], in_=ang[:], func=ACT.Sin)
         magnitude = keep.tile([P, pairs], F32)
-        phases = keep.tile([P, 2, pairs, 2], F32)
         nc.vector.scalar_tensor_tensor(
             out=magnitude[:], in0=ang[:], scalar=-1.0, in1=ang[:], op0=ALU.mult, op1=ALU.max
         )
-        nc.vector.tensor_tensor(
-            out=phases[:, 1],
-            in0=ang[:].unsqueeze(2).to_broadcast([P, pairs, 2]),
-            in1=signs[:].unsqueeze(1).to_broadcast([P, pairs, 2]),
-            op=ALU.mult,
-        )
+        complement = keep.tile([P, pairs], F32)
         nc.vector.tensor_scalar(
-            out=phases[:, 0],
-            in0=magnitude[:].unsqueeze(2).to_broadcast([P, pairs, 2]),
+            out=complement[:],
+            in0=magnitude[:],
             scalar1=-1.0,
             scalar2=math.pi / 2,
             op0=ALU.mult,
             op1=ALU.add,
         )
-        trig = keep.tile([P, 2, TILES, HD], F32)
+        cosine = keep.tile([P, TILES, HD // 2, 2], F32)
         nc.scalar.activation(
-            out=trig[:].rearrange("p a j d -> p (a j d)"),
-            in_=phases[:].rearrange("p a i e -> p (a i e)"),
+            out=cosine[:].rearrange("p j i e -> p (j i) e"),
+            in_=complement[:].unsqueeze(2).to_broadcast([P, pairs, 2]),
             func=ACT.Sin,
+        )
+        signed_sine = keep.tile([P, TILES, HD // 2, 2], F32)
+        nc.vector.tensor_tensor(
+            out=signed_sine[:].rearrange("p j i e -> p (j i) e"),
+            in0=sine[:].unsqueeze(2).to_broadcast([P, pairs, 2]),
+            in1=signs[:].unsqueeze(1).to_broadcast([P, pairs, 2]),
+            op=ALU.mult,
         )
 
         grouped_w = {}
@@ -118,15 +128,19 @@ def tile_groupqueryatention_pa_kernel(tc, x, angles, wq, wk, wv, out_0, out_1, o
 
         def share(c, g):
             if c == 0:
-                return HEAD_SHARE
-            if (c, g) == (1, 0):
-                return BRIDGE_SHARE
+                return HEAD_SHARE if g < PASSES - 1 else HEAD_LAST_SHARE
+            if c == 1:
+                return BRIDGE_SHARE if g == PASSES - 1 else 0
+            if c == 5:
+                return TAIL_SHARE if g == EARLY - 1 else 0
+            if c == 6:
+                return 0
             return STEADY_SHARE if g == PASSES - 1 else 0
 
         def grouped_tile(c, g):
             if (c, g) not in grouped_w:
                 grouped_w[c, g] = grouped_pool.tile(
-                    [P, CHUNK, PACK], BF16, name="grouped", tag="grouped", align_bytes=64
+                    [P, widths[c], PACK], BF16, name="grouped", tag="grouped", align_bytes=64
                 )
             return grouped_w[c, g]
 
@@ -140,12 +154,12 @@ def tile_groupqueryatention_pa_kernel(tc, x, angles, wq, wk, wv, out_0, out_1, o
             nc.vector.tensor_copy(out=dst, in_=src)
 
         def interleave_scalar(c, g):
-            dst, src = interleave_views(c, g, share(c, g), CHUNK)
+            dst, src = interleave_views(c, g, share(c, g), widths[c])
             nc.scalar.copy(out=dst, in_=src)
 
         def quantize_w(c, g):
-            codes = codes_pool.tile([P, CHUNK], U32, name="w_codes", tag="w_codes", align_bytes=64)
-            scales = codes_pool.tile([P, CHUNK], U8, name="w_scales", tag="w_scales", align_bytes=64)
+            codes = codes_pool.tile([P, widths[c]], U32, name="w_codes", tag="w_codes", align_bytes=64)
+            scales = codes_pool.tile([P, widths[c]], U8, name="w_scales", tag="w_scales", align_bytes=64)
             nc.vector.quantize_mx(
                 out=codes[:].bitcast(E4M3X4),
                 scales=scales[:],
@@ -179,7 +193,7 @@ def tile_groupqueryatention_pa_kernel(tc, x, angles, wq, wk, wv, out_0, out_1, o
 
         def multiply(c, g, j):
             if g == 0:
-                acc[c, j] = psum.tile([P, CHUNK], F32, name="acc", tag="bank%d" % (TILES * (c % 2) + j))
+                acc[c, j] = psum.tile([P, widths[c]], F32, name="acc", tag="bank%d" % (TILES * bank_set[c] + j))
             x_codes, x_scales = codes_x[j]
             w_codes, w_scales = codes_w[c, g]
             cols = slice(g * P, (g + 1) * P)
@@ -199,13 +213,13 @@ def tile_groupqueryatention_pa_kernel(tc, x, angles, wq, wk, wv, out_0, out_1, o
                 multiply(c, g, j)
 
         def stage_tile(c):
-            stage[c] = keep.tile([P, HEADS, TILES, HD], F32, name="stage_%d" % c)
+            stage[c] = keep.tile([P, widths[c] // HD, TILES, HD], F32, name="stage_%d" % c)
 
         def rope_products(c, j):
             shape = [P, HEADS, HD // 2, 2]
             sums = acc[c, j][:].rearrange("p (h i e) -> p h i e", h=HEADS, e=2)
-            cos = trig[:, 0, j, :].rearrange("p (i e) -> p i e", e=2).unsqueeze(1).to_broadcast(shape)
-            sin = trig[:, 1, j, :].rearrange("p (i e) -> p i e", e=2).unsqueeze(1).to_broadcast(shape)
+            cos = cosine[:, j].unsqueeze(1).to_broadcast(shape)
+            sin = signed_sine[:, j].unsqueeze(1).to_broadcast(shape)
             nc.vector.tensor_tensor(
                 out=stage[c][:, :, j, :].rearrange("p h (i e) -> p h i e", e=2),
                 in0=sums,
@@ -230,70 +244,78 @@ def tile_groupqueryatention_pa_kernel(tc, x, angles, wq, wk, wv, out_0, out_1, o
                 in_=stage[c][:, :, tiles, :].rearrange("p h j d -> p h (j d)"),
             )
 
-        interleave_vector(0, 0)
-        interleave_scalar(0, 0)
-        quantize_w(0, 0)
-        transpose_x(0)
-        for s in range(1, PASSES):
-            transpose_x(s)
+        for s in range(PASSES):
             interleave_vector(0, s)
             interleave_scalar(0, s)
-            quantize_x(s - 1)
+            transpose_x(s)
             quantize_w(0, s)
-        quantize_x(TILES - 1)
-        interleave_vector(1, 0)
+            quantize_x(s)
         interleave_scalar(1, 0)
-        for j in range(2):
-            for g in range(PASSES - 1):
-                multiply(0, g, j)
-        for j in range(2):
-            multiply(0, PASSES - 1, j)
-        for j in range(2, TILES):
+        for j in range(TILES):
             for g in range(PASSES):
                 multiply(0, g, j)
-        quantize_and_multiply(1, 0)
 
-        def rope_run(c):
-            interleave_scalar(c + 1, 1)
-            interleave_scalar(c + 1, 2)
+        def rope_run(c, after_tile=None):
             stage_tile(c)
             for j in range(TILES):
                 rope_products(c, j)
+                if after_tile:
+                    after_tile(j)
                 if j < POOL_TILES:
                     rope_add(nc.gpsimd, c, slice(j, j + 1))
 
-        for c in range(1, CHUNKS - 1):
+        for c in range(1, 5):
             done = c - 1
+            interleave_scalar(c, 1)
+            interleave_scalar(c, 2)
             rope_run(done)
-            quantize_and_multiply(c, 1)
+            if c == 1:
+                quantize_and_multiply(c, 0)
+            quantize_w(c, 1)
             interleave_vector(c, 3)
             interleave_scalar(c, 3)
             quantize_w(c, 2)
             quantize_w(c, 3)
             for j in range(TILES):
-                multiply(c, 2, j)
-                multiply(c, 3, j)
+                for g in range(1, PASSES):
+                    multiply(c, g, j)
             rope_add(nc.vector, done, slice(POOL_TILES, TILES))
             store(done, slice(0, TILES))
-            interleave_scalar(c + 1, 0)
-            quantize_and_multiply(c + 1, 0)
+            if c < 4:
+                interleave_scalar(c + 1, 0)
+                quantize_and_multiply(c + 1, 0)
 
-        c = CHUNKS - 1
-        done = c - 1
-        rope_run(done)
+        def evacuate(engine_copy, c, j):
+            engine_copy(out=stage[c][:, :, j, :], in_=acc[c, j][:].rearrange("p (h d) -> p h d", d=HD))
+
+        done, first, second = 4, 5, 6
+        for g in range(EARLY):
+            if share(first, g):
+                interleave_vector(first, g)
+        for g in range(EARLY):
+            interleave_scalar(first, g)
+            quantize_w(first, g)
+
+        def early_passes(j):
+            for g in range(EARLY):
+                multiply(first, g, j)
+
+        rope_run(done, early_passes)
         store(done, slice(0, POOL_TILES))
-        quantize_and_multiply(c, 1)
-        rope_add(nc.vector, done, slice(POOL_TILES, TILES))
-        store(done, slice(POOL_TILES, TILES))
-        interleave_vector(c, 3)
-        interleave_scalar(c, 3)
-        quantize_and_multiply(c, 2)
-        quantize_and_multiply(c, 3)
-        stage_tile(c)
+        units = [(first, g) for g in range(EARLY, PASSES)] + [(second, g) for g in range(PASSES)]
+        stage_tile(first)
+        stage_tile(second)
+        for i, (c, g) in enumerate(units):
+            if i == ADDAT:
+                rope_add(nc.vector, done, slice(POOL_TILES, TILES))
+                store(done, slice(POOL_TILES, TILES))
+            interleave_scalar(c, g)
+            quantize_and_multiply(c, g)
+            if (c, g) == (second, EVAT):
+                for j in range(TILES):
+                    evacuate(nc.scalar.copy, first, j)
+                store(first, slice(0, TILES))
         for j in range(TILES):
-            sums = acc[c, j][:].rearrange("p (h d) -> p h d", h=HEADS)
-            if j % 2 == 0:
-                nc.scalar.copy(out=stage[c][:, :, j, :], in_=sums)
-            else:
-                nc.vector.tensor_copy(out=stage[c][:, :, j, :], in_=sums)
-                store(c, slice(j - 1, j + 1))
+            evacuate(nc.vector.tensor_copy if j % 2 == 0 else nc.scalar.copy, second, j)
+            if j % 2 == 1:
+                store(second, slice(j - 1, j + 1))

@@ -34,7 +34,7 @@ GB = 6
 ADDAT = 2
 EVAT = 3
 EARLY = 3
-STEADY_SHARE = 192
+STEADY_SHARE = 256
 POOL_TILES = 2
 
 
@@ -247,9 +247,11 @@ def tile_groupqueryatention_pa_kernel(tc, x, angles, wq, wk, wv, out_0, out_1, o
         for s in range(PASSES):
             interleave_vector(0, s)
             interleave_scalar(0, s)
+            if s > 0:
+                quantize_x(s - 1)
             transpose_x(s)
             quantize_w(0, s)
-            quantize_x(s)
+        quantize_x(3)
         interleave_scalar(1, 0)
         for j in range(TILES):
             for g in range(PASSES):

@@ -13,43 +13,45 @@ E5M2X4 = mybir.dt.float8_e5m2_x4
 ALU = mybir.AluOpType
 ACT = mybir.ActivationFunctionType
 
-T, C, HD = 512, 2048, 128
-FLOPS = 2 * T * C * 3072
+TOKENS, K_ALL, HEAD_DIM = 512, 2048, 128
+FLOPS = 2 * TOKENS * K_ALL * (2048 + 512 + 512)
 
 P = 128
 PACK = 4
 K_PASS = P * PACK
-PASSES = C // K_PASS
-TILES = T // P
-CHUNK = 512
-HEADS = CHUNK // HD
-CHUNKS = 6
-RUN = 4
+PASSES = K_ALL // K_PASS
+LAST_PASS = PASSES - 1
+TILES = TOKENS // P
+BANK = 512
+HEADS = BANK // HEAD_DIM
+PAIRS = HEAD_DIM // 2
 
-HEAD_SHARE = 320
-BRIDGE_SHARE = 384
-HEAD_LAST_SHARE = 384
-TAIL_SHARE = 128
-GB = 6
-ADDAT = 2
-EVAT = 3
-EARLY = 3
-STEADY_SHARE = 256
+K_CHUNK, FIRST_Q, LAST_Q, V_LOW, V_HIGH = 0, 1, 4, 5, 6
+WIDTHS = [BANK] * V_LOW + [BANK // 2] * 2
+BANK_SET = [c % 2 for c in range(V_LOW)] + [LAST_Q % 2, 1 - LAST_Q % 2]
+
+COLUMN_RUN = 4
+K_SHARE = 320
+K_LAST_SHARE = 384
+FIRST_Q_SHARE = 384
+Q_SHARE = 192
 POOL_TILES = 2
+V_EARLY = 2
+GROUPED_BUFS = 6
+CODES_BUFS = 6
 
 
 def tile_groupqueryatention_pa_kernel(tc, x, angles, wq, wk, wv, out_0, out_1, out_2):
     nc = tc.nc
-    x_rows = x[0].rearrange("(p j) k -> j p k", j=TILES)
-    dests = [out_1[0]] + [out_0[0, HEADS * i : HEADS * (i + 1)] for i in range(4)]
-    dests += [out_2[0, 0:2], out_2[0, 2:4]]
-    bank_set = [0, 1, 0, 1, 0, 0, 1]
-    widths = [CHUNK] * 5 + [CHUNK // 2] * 2
+    x_tiles = x[0].rearrange("(p j) k -> j p k", j=TILES)
+    dests = [out_1[0]]
+    dests += [out_0[0, HEADS * i : HEADS * (i + 1)] for i in range(LAST_Q - FIRST_Q + 1)]
+    dests += [out_2[0, : HEADS // 2], out_2[0, HEADS // 2 :]]
 
     with ExitStack() as ctx:
         keep = ctx.enter_context(tc.tile_pool(name="keep", bufs=1))
-        grouped_pool = ctx.enter_context(tc.tile_pool(name="grouped", bufs=GB))
-        codes_pool = ctx.enter_context(tc.tile_pool(name="codes", bufs=6))
+        grouped_pool = ctx.enter_context(tc.tile_pool(name="grouped", bufs=GROUPED_BUFS))
+        codes_pool = ctx.enter_context(tc.tile_pool(name="codes", bufs=CODES_BUFS))
         psum = ctx.enter_context(tc.psum_pool(name="psum", bufs=1))
         ctx.enter_context(tc.manual_schedule())
 
@@ -57,45 +59,45 @@ def tile_groupqueryatention_pa_kernel(tc, x, angles, wq, wk, wv, out_0, out_1, o
         raw_x = {}
 
         def load_w(w, g, col0, chunks):
-            width = sum(widths[c] for c in chunks)
+            width = sum(WIDTHS[c] for c in chunks)
             raw = keep.tile([P, PACK, width], BF16, name="raw_w_%d_%d" % (chunks[0], g))
             rows = w[g * K_PASS : (g + 1) * K_PASS, col0 : col0 + width]
             nc.sync.dma_start(out=raw[:], in_=rows.rearrange("(p t) n -> p t n", t=PACK))
             for i, c in enumerate(chunks):
-                raw_w[c, g] = raw[:, :, i * widths[c] : (i + 1) * widths[c]]
+                raw_w[c, g] = raw[:, :, i * WIDTHS[c] : (i + 1) * WIDTHS[c]]
 
         def load_x(j):
-            raw = keep.tile([P, C], BF16, name="raw_x_%d" % j)
-            nc.sync.dma_start(out=raw[:], in_=x_rows[j])
+            raw = keep.tile([P, K_ALL], BF16, name="raw_x_%d" % j)
+            nc.sync.dma_start(out=raw[:], in_=x_tiles[j])
             raw_x[j] = raw
 
-        ang = keep.tile([P, TILES * HD // 2], BF16)
-        nc.sync.dma_start(out=ang[:], in_=angles.rearrange("(p j) i -> p (j i)", j=TILES))
-        for s in range(PASSES):
-            load_x(s)
-            load_w(wk, s, 0, [0])
-        for c in (1, 2):
+        angle = keep.tile([P, TILES * PAIRS], BF16)
+        nc.sync.dma_start(out=angle[:], in_=angles.rearrange("(p j) i -> p (j i)", j=TILES))
+        for step in range(PASSES):
+            load_x(step)
+            load_w(wk, step, 0, [K_CHUNK])
+        for c in (FIRST_Q, FIRST_Q + 1):
             for g in range(PASSES):
-                load_w(wq, g, (c - 1) * CHUNK, [c])
+                load_w(wq, g, (c - FIRST_Q) * BANK, [c])
         for g in range(PASSES):
-            load_w(wq, g, 2 * CHUNK, [3, 4])
+            load_w(wq, g, 2 * BANK, [LAST_Q - 1, LAST_Q])
         for g in range(PASSES):
-            load_w(wv, g, 0, [5, 6])
+            load_w(wv, g, 0, [V_LOW, V_HIGH])
 
         ident = keep.tile([P, P], F32)
         make_identity(nc, ident[:])
 
-        pairs = TILES * HD // 2
+        all_pairs = TILES * PAIRS
         signs = keep.tile([P, 2], F32)
         nc.vector.memset(signs[:, 0:1], -1.0)
         nc.vector.memset(signs[:, 1:2], 1.0)
-        sine = keep.tile([P, pairs], F32)
-        nc.scalar.activation(out=sine[:], in_=ang[:], func=ACT.Sin)
-        magnitude = keep.tile([P, pairs], F32)
+        sine = keep.tile([P, all_pairs], F32)
+        nc.scalar.activation(out=sine[:], in_=angle[:], func=ACT.Sin)
+        magnitude = keep.tile([P, all_pairs], F32)
         nc.vector.scalar_tensor_tensor(
-            out=magnitude[:], in0=ang[:], scalar=-1.0, in1=ang[:], op0=ALU.mult, op1=ALU.max
+            out=magnitude[:], in0=angle[:], scalar=-1.0, in1=angle[:], op0=ALU.mult, op1=ALU.max
         )
-        complement = keep.tile([P, pairs], F32)
+        complement = keep.tile([P, all_pairs], F32)
         nc.vector.tensor_scalar(
             out=complement[:],
             in0=magnitude[:],
@@ -104,17 +106,17 @@ def tile_groupqueryatention_pa_kernel(tc, x, angles, wq, wk, wv, out_0, out_1, o
             op0=ALU.mult,
             op1=ALU.add,
         )
-        cosine = keep.tile([P, TILES, HD // 2, 2], F32)
+        cos_table = keep.tile([P, TILES, PAIRS, 2], F32)
         nc.scalar.activation(
-            out=cosine[:].rearrange("p j i e -> p (j i) e"),
-            in_=complement[:].unsqueeze(2).to_broadcast([P, pairs, 2]),
+            out=cos_table[:].rearrange("p j i e -> p (j i) e"),
+            in_=complement[:].unsqueeze(2).to_broadcast([P, all_pairs, 2]),
             func=ACT.Sin,
         )
-        signed_sine = keep.tile([P, TILES, HD // 2, 2], F32)
+        sin_table = keep.tile([P, TILES, PAIRS, 2], F32)
         nc.vector.tensor_tensor(
-            out=signed_sine[:].rearrange("p j i e -> p (j i) e"),
-            in0=sine[:].unsqueeze(2).to_broadcast([P, pairs, 2]),
-            in1=signs[:].unsqueeze(1).to_broadcast([P, pairs, 2]),
+            out=sin_table[:].rearrange("p j i e -> p (j i) e"),
+            in0=sine[:].unsqueeze(2).to_broadcast([P, all_pairs, 2]),
+            in1=signs[:].unsqueeze(1).to_broadcast([P, all_pairs, 2]),
             op=ALU.mult,
         )
 
@@ -122,44 +124,36 @@ def tile_groupqueryatention_pa_kernel(tc, x, angles, wq, wk, wv, out_0, out_1, o
         codes_w = {}
         grouped_x = {}
         codes_x = {}
-        acc = {}
+        sums = {}
         stage = {}
-        swapped = keep.tile([P, HEADS, TILES, HD], F32)
+        sin_terms = keep.tile([P, HEADS, TILES, HEAD_DIM], F32)
 
-        def share(c, g):
-            if c == 0:
-                return HEAD_SHARE if g < PASSES - 1 else HEAD_LAST_SHARE
-            if c == 1:
-                return BRIDGE_SHARE if g == PASSES - 1 else 0
-            if c == 5:
-                return TAIL_SHARE if g == EARLY - 1 else 0
-            if c == 6:
+        def vector_share(c, g):
+            if c == K_CHUNK:
+                return K_SHARE if g < LAST_PASS else K_LAST_SHARE
+            if c > LAST_Q or g < LAST_PASS:
                 return 0
-            return STEADY_SHARE if g == PASSES - 1 else 0
+            return FIRST_Q_SHARE if c == FIRST_Q else Q_SHARE
 
-        def grouped_tile(c, g):
+        def interleave(copy, c, g, col0, col1):
             if (c, g) not in grouped_w:
                 grouped_w[c, g] = grouped_pool.tile(
-                    [P, widths[c], PACK], BF16, name="grouped", tag="grouped", align_bytes=64
+                    [P, WIDTHS[c], PACK], BF16, name="grouped", tag="grouped", align_bytes=64
                 )
-            return grouped_w[c, g]
-
-        def interleave_views(c, g, lo, hi):
-            dst = grouped_tile(c, g)[:, lo:hi, :].rearrange("p (n i) t -> p n t i", i=RUN)
-            src = raw_w[c, g][:, :, lo:hi].rearrange("p t (n i) -> p n t i", i=RUN)
-            return dst, src
+            copy(
+                out=grouped_w[c, g][:, col0:col1, :].rearrange("p (n i) t -> p n t i", i=COLUMN_RUN),
+                in_=raw_w[c, g][:, :, col0:col1].rearrange("p t (n i) -> p n t i", i=COLUMN_RUN),
+            )
 
         def interleave_vector(c, g):
-            dst, src = interleave_views(c, g, 0, share(c, g))
-            nc.vector.tensor_copy(out=dst, in_=src)
+            interleave(nc.vector.tensor_copy, c, g, 0, vector_share(c, g))
 
         def interleave_scalar(c, g):
-            dst, src = interleave_views(c, g, share(c, g), widths[c])
-            nc.scalar.copy(out=dst, in_=src)
+            interleave(nc.scalar.copy, c, g, vector_share(c, g), WIDTHS[c])
 
         def quantize_w(c, g):
-            codes = codes_pool.tile([P, widths[c]], U32, name="w_codes", tag="w_codes", align_bytes=64)
-            scales = codes_pool.tile([P, widths[c]], U8, name="w_scales", tag="w_scales", align_bytes=64)
+            codes = codes_pool.tile([P, WIDTHS[c]], U32, name="w_codes", tag="w_codes", align_bytes=64)
+            scales = codes_pool.tile([P, WIDTHS[c]], U8, name="w_scales", tag="w_scales", align_bytes=64)
             nc.vector.quantize_mx(
                 out=codes[:].bitcast(E4M3X4),
                 scales=scales[:],
@@ -169,20 +163,22 @@ def tile_groupqueryatention_pa_kernel(tc, x, angles, wq, wk, wv, out_0, out_1, o
 
         def transpose_x(j):
             words = raw_x[j][:].bitcast(F32)
-            grouped = grouped_pool.tile([P, C], BF16, name="grouped", tag="grouped", align_bytes=64)
+            words_per_pass = K_PASS // 2
+            grouped = grouped_pool.tile([P, K_ALL], BF16, name="grouped", tag="grouped", align_bytes=64)
             grouped_x[j] = grouped
-            for b in range(2):
-                xt = psum.tile([P, 2, 2, P], F32, name="xt", tag="bank%d" % (TILES + 2 * (j % 2) + b))
-                for h in range(2):
-                    g = 2 * b + h
+            for half in range(2):
+                bank = TILES * BANK_SET[FIRST_Q] + 2 * (j % 2) + half
+                turned = psum.tile([P, 2, 2, P], F32, name="turned", tag="bank%d" % bank)
+                for slot in range(2):
+                    word0 = (2 * half + slot) * words_per_pass
                     for u in range(2):
                         nc.tensor.transpose(
-                            xt[:, h, u, :], words[:, 256 * g + u : 256 * (g + 1) : 2], ident[:]
+                            turned[:, slot, u, :], words[:, word0 + u : word0 + words_per_pass : 2], ident[:]
                         )
-                dst = grouped[:].bitcast(F32)[:, 512 * b : 512 * (b + 1)]
+                dst = grouped[:].bitcast(F32)[:, BANK * half : BANK * (half + 1)]
                 nc.scalar.copy(
-                    out=dst.rearrange("p (h r u) -> p h r u", h=2, u=2),
-                    in_=xt[:].rearrange("p h u r -> p h r u"),
+                    out=dst.rearrange("p (s r u) -> p s r u", s=2, u=2),
+                    in_=turned[:].rearrange("p s u r -> p s r u"),
                 )
 
         def quantize_x(j):
@@ -193,49 +189,60 @@ def tile_groupqueryatention_pa_kernel(tc, x, angles, wq, wk, wv, out_0, out_1, o
 
         def multiply(c, g, j):
             if g == 0:
-                acc[c, j] = psum.tile([P, widths[c]], F32, name="acc", tag="bank%d" % (TILES * bank_set[c] + j))
+                bank = TILES * BANK_SET[c] + j
+                sums[c, j] = psum.tile([P, WIDTHS[c]], F32, name="sums", tag="bank%d" % bank)
             x_codes, x_scales = codes_x[j]
             w_codes, w_scales = codes_w[c, g]
-            cols = slice(g * P, (g + 1) * P)
+            pass_cols = slice(g * P, (g + 1) * P)
             nc.tensor.matmul_mx(
-                out=acc[c, j][:],
-                lhsT=x_codes[:, cols].bitcast(E5M2X4),
-                lhsT_scale=x_scales[:, cols],
+                out=sums[c, j][:],
+                lhsT=x_codes[:, pass_cols].bitcast(E5M2X4),
+                lhsT_scale=x_scales[:, pass_cols],
                 rhs=w_codes[:].bitcast(E4M3X4),
                 rhs_scale=w_scales[:],
                 start=(g == 0),
-                stop=(g == PASSES - 1),
+                stop=(g == LAST_PASS),
             )
+
+        def multiply_passes(c, passes, j):
+            for g in passes:
+                multiply(c, g, j)
 
         def quantize_and_multiply(c, g):
             quantize_w(c, g)
             for j in range(TILES):
                 multiply(c, g, j)
 
-        def stage_tile(c):
-            stage[c] = keep.tile([P, widths[c] // HD, TILES, HD], F32, name="stage_%d" % c)
+        def new_stage(c):
+            stage[c] = keep.tile([P, WIDTHS[c] // HEAD_DIM, TILES, HEAD_DIM], F32, name="stage_%d" % c)
 
-        def rope_products(c, j):
-            shape = [P, HEADS, HD // 2, 2]
-            sums = acc[c, j][:].rearrange("p (h i e) -> p h i e", h=HEADS, e=2)
-            cos = cosine[:, j].unsqueeze(1).to_broadcast(shape)
-            sin = signed_sine[:, j].unsqueeze(1).to_broadcast(shape)
+        def rotation_products(c, j):
+            shape = [P, HEADS, PAIRS, 2]
+            pairs = sums[c, j][:].rearrange("p (h i e) -> p h i e", h=HEADS, e=2)
             nc.vector.tensor_tensor(
                 out=stage[c][:, :, j, :].rearrange("p h (i e) -> p h i e", e=2),
-                in0=sums,
-                in1=cos,
+                in0=pairs,
+                in1=cos_table[:, j].unsqueeze(1).to_broadcast(shape),
                 op=ALU.mult,
             )
             nc.vector.tensor_tensor(
-                out=swapped[:, :, j, :].rearrange("p h (i e) -> p h i e", e=2),
-                in0=sums[:, :, :, ::-1],
-                in1=sin,
+                out=sin_terms[:, :, j, :].rearrange("p h (i e) -> p h i e", e=2),
+                in0=pairs[:, :, :, ::-1],
+                in1=sin_table[:, j].unsqueeze(1).to_broadcast(shape),
                 op=ALU.mult,
             )
 
-        def rope_add(engine, c, tiles):
+        def rotation_add(engine, c, tiles):
             part = stage[c][:, :, tiles, :]
-            engine.tensor_tensor(out=part, in0=part, in1=swapped[:, :, tiles, :], op=ALU.add)
+            engine.tensor_tensor(out=part, in0=part, in1=sin_terms[:, :, tiles, :], op=ALU.add)
+
+        def rotate_tile(c, j):
+            rotation_products(c, j)
+            if j < POOL_TILES:
+                rotation_add(nc.gpsimd, c, slice(j, j + 1))
+
+        def copy_out(copy, c, j):
+            copy(out=stage[c][:, :, j, :], in_=sums[c, j][:].rearrange("p (h d) -> p h d", d=HEAD_DIM))
 
         def store(c, tiles):
             dst = dests[c].rearrange("h (p j) d -> p h j d", j=TILES)[:, :, tiles, :]
@@ -244,80 +251,67 @@ def tile_groupqueryatention_pa_kernel(tc, x, angles, wq, wk, wv, out_0, out_1, o
                 in_=stage[c][:, :, tiles, :].rearrange("p h j d -> p h (j d)"),
             )
 
-        for s in range(PASSES):
-            interleave_vector(0, s)
-            interleave_scalar(0, s)
-            if s > 0:
-                quantize_x(s - 1)
-            transpose_x(s)
-            quantize_w(0, s)
-        quantize_x(3)
-        interleave_scalar(1, 0)
+        pool_tiles = slice(0, POOL_TILES)
+        vector_tiles = slice(POOL_TILES, TILES)
+
+        for step in range(PASSES):
+            interleave_vector(K_CHUNK, step)
+            interleave_scalar(K_CHUNK, step)
+            if step > 0:
+                quantize_x(step - 1)
+            transpose_x(step)
+            quantize_w(K_CHUNK, step)
+        quantize_x(TILES - 1)
+        interleave_scalar(FIRST_Q, 0)
         for j in range(TILES):
-            for g in range(PASSES):
-                multiply(0, g, j)
+            multiply_passes(K_CHUNK, range(PASSES), j)
 
-        def rope_run(c, after_tile=None):
-            stage_tile(c)
-            for j in range(TILES):
-                rope_products(c, j)
-                if after_tile:
-                    after_tile(j)
-                if j < POOL_TILES:
-                    rope_add(nc.gpsimd, c, slice(j, j + 1))
-
-        for c in range(1, 5):
-            done = c - 1
+        for c in range(FIRST_Q, LAST_Q + 1):
+            rotated = c - 1
             interleave_scalar(c, 1)
             interleave_scalar(c, 2)
-            rope_run(done)
-            if c == 1:
+            new_stage(rotated)
+            for j in range(TILES):
+                rotate_tile(rotated, j)
+            if c == FIRST_Q:
                 quantize_and_multiply(c, 0)
             quantize_w(c, 1)
-            interleave_vector(c, 3)
-            interleave_scalar(c, 3)
+            interleave_vector(c, LAST_PASS)
+            interleave_scalar(c, LAST_PASS)
             quantize_w(c, 2)
-            quantize_w(c, 3)
+            quantize_w(c, LAST_PASS)
             for j in range(TILES):
-                for g in range(1, PASSES):
-                    multiply(c, g, j)
-            rope_add(nc.vector, done, slice(POOL_TILES, TILES))
-            store(done, slice(0, TILES))
-            if c < 4:
+                multiply_passes(c, range(1, PASSES), j)
+            rotation_add(nc.vector, rotated, vector_tiles)
+            store(rotated, slice(0, TILES))
+            if c < LAST_Q:
                 interleave_scalar(c + 1, 0)
                 quantize_and_multiply(c + 1, 0)
 
-        def evacuate(engine_copy, c, j):
-            engine_copy(out=stage[c][:, :, j, :], in_=acc[c, j][:].rearrange("p (h d) -> p h d", d=HD))
-
-        done, first, second = 4, 5, 6
-        for g in range(EARLY):
-            if share(first, g):
-                interleave_vector(first, g)
-        for g in range(EARLY):
-            interleave_scalar(first, g)
-            quantize_w(first, g)
-
-        def early_passes(j):
-            for g in range(EARLY):
-                multiply(first, g, j)
-
-        rope_run(done, early_passes)
-        store(done, slice(0, POOL_TILES))
-        units = [(first, g) for g in range(EARLY, PASSES)] + [(second, g) for g in range(PASSES)]
-        stage_tile(first)
-        stage_tile(second)
-        for i, (c, g) in enumerate(units):
-            if i == ADDAT:
-                rope_add(nc.vector, done, slice(POOL_TILES, TILES))
-                store(done, slice(POOL_TILES, TILES))
-            interleave_scalar(c, g)
-            quantize_and_multiply(c, g)
-            if (c, g) == (second, EVAT):
-                for j in range(TILES):
-                    evacuate(nc.scalar.copy, first, j)
-                store(first, slice(0, TILES))
+        for g in range(V_EARLY):
+            interleave_scalar(V_LOW, g)
+            quantize_w(V_LOW, g)
+        new_stage(LAST_Q)
         for j in range(TILES):
-            evacuate(nc.vector.tensor_copy if j % 2 == 0 else nc.scalar.copy, second, j)
-            if j % 2 == 1:
-                store(second, slice(j - 1, j + 1))
+            rotate_tile(LAST_Q, j)
+            multiply_passes(V_LOW, range(V_EARLY), j)
+        store(LAST_Q, pool_tiles)
+        new_stage(V_LOW)
+        new_stage(V_HIGH)
+        for g in range(V_EARLY, PASSES):
+            interleave_scalar(V_LOW, g)
+            quantize_and_multiply(V_LOW, g)
+        interleave_scalar(V_HIGH, 0)
+        quantize_and_multiply(V_HIGH, 0)
+        rotation_add(nc.vector, LAST_Q, vector_tiles)
+        store(LAST_Q, vector_tiles)
+        for g in range(1, PASSES):
+            interleave_scalar(V_HIGH, g)
+            quantize_and_multiply(V_HIGH, g)
+        for j in range(TILES):
+            copy_out(nc.scalar.copy, V_LOW, j)
+        store(V_LOW, slice(0, TILES))
+        for j in range(0, TILES, 2):
+            copy_out(nc.vector.tensor_copy, V_HIGH, j)
+            copy_out(nc.scalar.copy, V_HIGH, j + 1)
+            store(V_HIGH, slice(j, j + 2))

import math
from contextlib import ExitStack

import concourse.mybir as mybir
from concourse.masks import make_identity

F32 = mybir.dt.float32
BF16 = mybir.dt.bfloat16
U32 = mybir.dt.uint32
U8 = mybir.dt.uint8
E4M3X4 = mybir.dt.float8_e4m3fn_x4
E5M2X4 = mybir.dt.float8_e5m2_x4
ALU = mybir.AluOpType
ACT = mybir.ActivationFunctionType

TOKENS, K_ALL, HEAD_DIM = 512, 2048, 128
FLOPS = 2 * TOKENS * K_ALL * (2048 + 512 + 512)

P = 128
PACK = 4
K_PASS = P * PACK
PASSES = K_ALL // K_PASS
LAST_PASS = PASSES - 1
TILES = TOKENS // P
BANK = 512
HEADS = BANK // HEAD_DIM
PAIRS = HEAD_DIM // 2

K_CHUNK, FIRST_Q, LAST_Q, V_LOW, V_HIGH = 0, 1, 4, 5, 6
WIDTHS = [BANK] * V_LOW + [BANK // 2] * 2
BANK_SET = [c % 2 for c in range(V_LOW)] + [LAST_Q % 2, 1 - LAST_Q % 2]

COLUMN_RUN = 4
K_SHARE = 320
K_LAST_SHARE = 384
FIRST_Q_SHARE = 384
Q_SHARE = 192
POOL_TILES = 2
V_EARLY = 2
GROUPED_BUFS = 6
CODES_BUFS = 6


def tile_groupqueryatention_pa_kernel(tc, x, angles, wq, wk, wv, out_0, out_1, out_2):
    nc = tc.nc
    x_tiles = x[0].rearrange("(p j) k -> j p k", j=TILES)
    dests = [out_1[0]]
    dests += [out_0[0, HEADS * i : HEADS * (i + 1)] for i in range(LAST_Q - FIRST_Q + 1)]
    dests += [out_2[0, : HEADS // 2], out_2[0, HEADS // 2 :]]

    with ExitStack() as ctx:
        keep = ctx.enter_context(tc.tile_pool(name="keep", bufs=1))
        grouped_pool = ctx.enter_context(tc.tile_pool(name="grouped", bufs=GROUPED_BUFS))
        codes_pool = ctx.enter_context(tc.tile_pool(name="codes", bufs=CODES_BUFS))
        psum = ctx.enter_context(tc.psum_pool(name="psum", bufs=1))
        ctx.enter_context(tc.manual_schedule())

        raw_w = {}
        raw_x = {}

        def load_w(w, g, col0, chunks):
            width = sum(WIDTHS[c] for c in chunks)
            raw = keep.tile([P, PACK, width], BF16, name="raw_w_%d_%d" % (chunks[0], g))
            rows = w[g * K_PASS : (g + 1) * K_PASS, col0 : col0 + width]
            nc.sync.dma_start(out=raw[:], in_=rows.rearrange("(p t) n -> p t n", t=PACK))
            for i, c in enumerate(chunks):
                raw_w[c, g] = raw[:, :, i * WIDTHS[c] : (i + 1) * WIDTHS[c]]

        def load_x(j):
            raw = keep.tile([P, K_ALL], BF16, name="raw_x_%d" % j)
            nc.sync.dma_start(out=raw[:], in_=x_tiles[j])
            raw_x[j] = raw

        angle = keep.tile([P, TILES * PAIRS], BF16)
        nc.sync.dma_start(out=angle[:], in_=angles.rearrange("(p j) i -> p (j i)", j=TILES))
        for step in range(PASSES):
            load_x(step)
            load_w(wk, step, 0, [K_CHUNK])
        for c in (FIRST_Q, FIRST_Q + 1):
            for g in range(PASSES):
                load_w(wq, g, (c - FIRST_Q) * BANK, [c])
        for g in range(PASSES):
            load_w(wq, g, 2 * BANK, [LAST_Q - 1, LAST_Q])
        for g in range(PASSES):
            load_w(wv, g, 0, [V_LOW, V_HIGH])

        ident = keep.tile([P, P], F32)
        make_identity(nc, ident[:])

        all_pairs = TILES * PAIRS
        signs = keep.tile([P, 2], F32)
        nc.vector.memset(signs[:, 0:1], -1.0)
        nc.vector.memset(signs[:, 1:2], 1.0)
        sine = keep.tile([P, all_pairs], F32)
        nc.scalar.activation(out=sine[:], in_=angle[:], func=ACT.Sin)
        magnitude = keep.tile([P, all_pairs], F32)
        nc.vector.scalar_tensor_tensor(
            out=magnitude[:], in0=angle[:], scalar=-1.0, in1=angle[:], op0=ALU.mult, op1=ALU.max
        )
        complement = keep.tile([P, all_pairs], F32)
        nc.vector.tensor_scalar(
            out=complement[:],
            in0=magnitude[:],
            scalar1=-1.0,
            scalar2=math.pi / 2,
            op0=ALU.mult,
            op1=ALU.add,
        )
        cos_table = keep.tile([P, TILES, PAIRS, 2], F32)
        nc.scalar.activation(
            out=cos_table[:].rearrange("p j i e -> p (j i) e"),
            in_=complement[:].unsqueeze(2).to_broadcast([P, all_pairs, 2]),
            func=ACT.Sin,
        )
        sin_table = keep.tile([P, TILES, PAIRS, 2], F32)
        nc.vector.tensor_tensor(
            out=sin_table[:].rearrange("p j i e -> p (j i) e"),
            in0=sine[:].unsqueeze(2).to_broadcast([P, all_pairs, 2]),
            in1=signs[:].unsqueeze(1).to_broadcast([P, all_pairs, 2]),
            op=ALU.mult,
        )

        grouped_w = {}
        codes_w = {}
        grouped_x = {}
        codes_x = {}
        sums = {}
        stage = {}
        sin_terms = keep.tile([P, HEADS, TILES, HEAD_DIM], F32)

        def vector_share(c, g):
            if c == K_CHUNK:
                return K_SHARE if g < LAST_PASS else K_LAST_SHARE
            if c > LAST_Q or g < LAST_PASS:
                return 0
            return FIRST_Q_SHARE if c == FIRST_Q else Q_SHARE

        def interleave(copy, c, g, col0, col1):
            if (c, g) not in grouped_w:
                grouped_w[c, g] = grouped_pool.tile(
                    [P, WIDTHS[c], PACK], BF16, name="grouped", tag="grouped", align_bytes=64
                )
            copy(
                out=grouped_w[c, g][:, col0:col1, :].rearrange("p (n i) t -> p n t i", i=COLUMN_RUN),
                in_=raw_w[c, g][:, :, col0:col1].rearrange("p t (n i) -> p n t i", i=COLUMN_RUN),
            )

        def interleave_vector(c, g):
            interleave(nc.vector.tensor_copy, c, g, 0, vector_share(c, g))

        def interleave_scalar(c, g):
            interleave(nc.scalar.copy, c, g, vector_share(c, g), WIDTHS[c])

        def quantize_w(c, g):
            codes = codes_pool.tile([P, WIDTHS[c]], U32, name="w_codes", tag="w_codes", align_bytes=64)
            scales = codes_pool.tile([P, WIDTHS[c]], U8, name="w_scales", tag="w_scales", align_bytes=64)
            nc.vector.quantize_mx(
                out=codes[:].bitcast(E4M3X4),
                scales=scales[:],
                in_=grouped_w[c, g][:].rearrange("p n t -> p (n t)"),
            )
            codes_w[c, g] = (codes, scales)

        def transpose_x(j):
            words = raw_x[j][:].bitcast(F32)
            words_per_pass = K_PASS // 2
            grouped = grouped_pool.tile([P, K_ALL], BF16, name="grouped", tag="grouped", align_bytes=64)
            grouped_x[j] = grouped
            for half in range(2):
                bank = TILES * BANK_SET[FIRST_Q] + 2 * (j % 2) + half
                turned = psum.tile([P, 2, 2, P], F32, name="turned", tag="bank%d" % bank)
                for slot in range(2):
                    word0 = (2 * half + slot) * words_per_pass
                    for u in range(2):
                        nc.tensor.transpose(
                            turned[:, slot, u, :], words[:, word0 + u : word0 + words_per_pass : 2], ident[:]
                        )
                dst = grouped[:].bitcast(F32)[:, BANK * half : BANK * (half + 1)]
                nc.scalar.copy(
                    out=dst.rearrange("p (s r u) -> p s r u", s=2, u=2),
                    in_=turned[:].rearrange("p s u r -> p s r u"),
                )

        def quantize_x(j):
            codes = keep.tile([P, PASSES * P], U32, name="x_codes_%d" % j, align_bytes=64)
            scales = keep.tile([P, PASSES * P], U8, name="x_scales_%d" % j, align_bytes=64)
            nc.vector.quantize_mx(out=codes[:].bitcast(E5M2X4), scales=scales[:], in_=grouped_x[j][:])
            codes_x[j] = (codes, scales)

        def multiply(c, g, j):
            if g == 0:
                bank = TILES * BANK_SET[c] + j
                sums[c, j] = psum.tile([P, WIDTHS[c]], F32, name="sums", tag="bank%d" % bank)
            x_codes, x_scales = codes_x[j]
            w_codes, w_scales = codes_w[c, g]
            pass_cols = slice(g * P, (g + 1) * P)
            nc.tensor.matmul_mx(
                out=sums[c, j][:],
                lhsT=x_codes[:, pass_cols].bitcast(E5M2X4),
                lhsT_scale=x_scales[:, pass_cols],
                rhs=w_codes[:].bitcast(E4M3X4),
                rhs_scale=w_scales[:],
                start=(g == 0),
                stop=(g == LAST_PASS),
            )

        def multiply_passes(c, passes, j):
            for g in passes:
                multiply(c, g, j)

        def quantize_and_multiply(c, g):
            quantize_w(c, g)
            for j in range(TILES):
                multiply(c, g, j)

        def new_stage(c):
            stage[c] = keep.tile([P, WIDTHS[c] // HEAD_DIM, TILES, HEAD_DIM], F32, name="stage_%d" % c)

        def rotation_products(c, j):
            shape = [P, HEADS, PAIRS, 2]
            pairs = sums[c, j][:].rearrange("p (h i e) -> p h i e", h=HEADS, e=2)
            nc.vector.tensor_tensor(
                out=stage[c][:, :, j, :].rearrange("p h (i e) -> p h i e", e=2),
                in0=pairs,
                in1=cos_table[:, j].unsqueeze(1).to_broadcast(shape),
                op=ALU.mult,
            )
            nc.vector.tensor_tensor(
                out=sin_terms[:, :, j, :].rearrange("p h (i e) -> p h i e", e=2),
                in0=pairs[:, :, :, ::-1],
                in1=sin_table[:, j].unsqueeze(1).to_broadcast(shape),
                op=ALU.mult,
            )

        def rotation_add(engine, c, tiles):
            part = stage[c][:, :, tiles, :]
            engine.tensor_tensor(out=part, in0=part, in1=sin_terms[:, :, tiles, :], op=ALU.add)

        def rotate_tile(c, j):
            rotation_products(c, j)
            if j < POOL_TILES:
                rotation_add(nc.gpsimd, c, slice(j, j + 1))

        def copy_out(copy, c, j):
            copy(out=stage[c][:, :, j, :], in_=sums[c, j][:].rearrange("p (h d) -> p h d", d=HEAD_DIM))

        def store(c, tiles):
            dst = dests[c].rearrange("h (p j) d -> p h j d", j=TILES)[:, :, tiles, :]
            nc.sync.dma_start(
                out=dst.rearrange("p h j d -> p h (j d)"),
                in_=stage[c][:, :, tiles, :].rearrange("p h j d -> p h (j d)"),
            )

        pool_tiles = slice(0, POOL_TILES)
        vector_tiles = slice(POOL_TILES, TILES)

        for step in range(PASSES):
            interleave_vector(K_CHUNK, step)
            interleave_scalar(K_CHUNK, step)
            if step > 0:
                quantize_x(step - 1)
            transpose_x(step)
            quantize_w(K_CHUNK, step)
        quantize_x(TILES - 1)
        interleave_scalar(FIRST_Q, 0)
        for j in range(TILES):
            multiply_passes(K_CHUNK, range(PASSES), j)

        for c in range(FIRST_Q, LAST_Q + 1):
            rotated = c - 1
            interleave_scalar(c, 1)
            interleave_scalar(c, 2)
            new_stage(rotated)
            for j in range(TILES):
                rotate_tile(rotated, j)
            if c == FIRST_Q:
                quantize_and_multiply(c, 0)
            quantize_w(c, 1)
            interleave_vector(c, LAST_PASS)
            interleave_scalar(c, LAST_PASS)
            quantize_w(c, 2)
            quantize_w(c, LAST_PASS)
            for j in range(TILES):
                multiply_passes(c, range(1, PASSES), j)
            rotation_add(nc.vector, rotated, vector_tiles)
            store(rotated, slice(0, TILES))
            if c < LAST_Q:
                interleave_scalar(c + 1, 0)
                quantize_and_multiply(c + 1, 0)

        for g in range(V_EARLY):
            interleave_scalar(V_LOW, g)
            quantize_w(V_LOW, g)
        new_stage(LAST_Q)
        for j in range(TILES):
            rotate_tile(LAST_Q, j)
            multiply_passes(V_LOW, range(V_EARLY), j)
        store(LAST_Q, pool_tiles)
        new_stage(V_LOW)
        new_stage(V_HIGH)
        for g in range(V_EARLY, PASSES):
            interleave_scalar(V_LOW, g)
            quantize_and_multiply(V_LOW, g)
        interleave_scalar(V_HIGH, 0)
        quantize_and_multiply(V_HIGH, 0)
        rotation_add(nc.vector, LAST_Q, vector_tiles)
        store(LAST_Q, vector_tiles)
        for g in range(1, PASSES):
            interleave_scalar(V_HIGH, g)
            quantize_and_multiply(V_HIGH, g)
        for j in range(TILES):
            copy_out(nc.scalar.copy, V_LOW, j)
        store(V_LOW, slice(0, TILES))
        for j in range(0, TILES, 2):
            copy_out(nc.vector.tensor_copy, V_HIGH, j)
            copy_out(nc.scalar.copy, V_HIGH, j + 1)
            store(V_HIGH, slice(j, j + 2))
